import numpy as np
import ml_dtypes


def mxq(x, axis, fmt="e4m3"):
    dtype, down = {"e4m3": (ml_dtypes.float8_e4m3fn, 7), "e5m2": (ml_dtypes.float8_e5m2, 14)}[fmt]
    v = np.moveaxis(np.asarray(x, np.float32).astype(ml_dtypes.bfloat16).astype(np.float64), axis, -1)
    blocks = v.reshape(v.shape[:-1] + (-1, 32))
    amax = np.abs(blocks).max(-1, keepdims=True)
    byte = np.maximum(np.where(amax > 0, np.frexp(amax)[1] - 1 + 127, 0) - down, 1)
    scale = np.exp2(byte - 127.0)
    codes = (blocks / scale).astype(np.float32).astype(dtype).astype(np.float64)
    return np.moveaxis((codes * scale).reshape(v.shape), -1, axis)


WIDE = False


def mx_kscale(k):
    if not WIDE:
        return np.ones(k)
    levels = np.array([10, -10, 5, -5, 0])
    a = np.random.permutation(np.resize(levels, k // 512 * 4)).reshape(k // 512, 4)
    idx = np.arange(k)
    return np.exp2(a[idx // 512, idx % 128 // 32])


BF16 = ml_dtypes.bfloat16


def bf(x):
    return np.asarray(x, np.float32).astype(BF16)


def f64(x):
    return np.asarray(x).astype(np.float64)


E2M1 = np.array([0.0, 0.5, 1.0, 1.5, 2.0, 3.0, 4.0, 6.0, -0.0, -0.5, -1.0, -1.5, -2.0, -3.0, -4.0, -6.0])


def pack_weight(w, fmt):
    k, n = w.shape
    w = f64(bf(w)).reshape(k // 32, 32, n)
    amax = np.abs(w).max(1)
    if fmt == "e4m3":
        byte = np.frexp(amax)[1] - 1 + 127 - 7
    else:
        mant, ex = np.frexp(amax / 6.0)
        byte = np.where(mant > 0.5, ex, ex - 1) + 127
    byte = np.clip(np.where(amax > 0, byte, 1), 1, 254)
    scaled = (w * np.exp2(127.0 - byte)[:, None, :]).reshape(k, n).astype(np.float32)
    by_word = np.ascontiguousarray(scaled.reshape(k // 512, 128, 4, n).transpose(0, 1, 3, 2))
    if fmt == "e4m3":
        words = by_word.astype(ml_dtypes.float8_e4m3fn).view(np.uint8)
    else:
        c = by_word.astype(ml_dtypes.float4_e2m1fn).view(np.uint8) & 0xF
        words = c[..., 0::2] | (c[..., 1::2] << 4)
    return np.ascontiguousarray(words), np.ascontiguousarray(byte.astype(np.uint8).reshape(k // 512, 16, n))


def unpack_weight(words, scales, fmt):
    g, p, n, _ = words.shape
    if fmt == "e4m3":
        vals = np.ascontiguousarray(words).view(ml_dtypes.float8_e4m3fn).astype(np.float64)
    else:
        nib = np.empty((g, p, n, 4), np.uint8)
        nib[..., 0::2] = words & 0xF
        nib[..., 1::2] = words >> 4
        vals = E2M1[nib]
    vals = vals * np.repeat(np.exp2(scales.astype(np.float64) - 127.0), 8, axis=1)[..., None]
    return vals.transpose(0, 1, 3, 2).reshape(g * 512, n)

def pack4(w):
    words, scales = pack_weight(w, "e2m1")
    return words.reshape(words.shape[0], 128, -1), scales


def unpack4(words, scales):
    return unpack_weight(words.reshape(words.shape[0], 128, -1, 2), scales, "e2m1")


B, M, F, U = 256, 16, 512, 512


def setup_inputs():
    s = mx_kscale(F)
    limit = np.sqrt(6.0 / (F + U))
    x = bf(np.random.standard_normal((B, M, F)) * s)
    stack = np.random.uniform(-limit, limit, (M, F, U)) / s[None, :, None]
    words, scales = pack4(stack.reshape(-1, U))
    b = bf(np.random.standard_normal((M, U)) * 0.1)
    return {"x": x, "W_words": words, "W_scales": scales, "b": b}


def reference(x, W_words, W_scales, b):
    xq = mxq(f64(x), 2, "e4m3")
    wq = unpack4(W_words, W_scales).reshape(M, F, U)
    y = (xq.transpose(1, 0, 2) @ wq).transpose(1, 0, 2)
    y = np.maximum(y + f64(b)[None, :, :], 0.0)
    return y.reshape(y.shape[0], -1)

@@ -1,0 +1,176 @@
+from contextlib import ExitStack
+
+import concourse.mybir as mybir
+from concourse.masks import make_identity
+
+F32 = mybir.dt.float32
+BF16 = mybir.dt.bfloat16
+I32 = mybir.dt.int32
+U32 = mybir.dt.uint32
+U8 = mybir.dt.uint8
+FP8X4 = mybir.dt.float8_e4m3fn_x4
+FP4X4 = mybir.dt.float4_e2m1fn_x4
+
+P = 128
+PACK = 4
+BATCH = 256
+MASKS = 16
+K = 512
+N = 512
+ROW_TILES = BATCH // P
+GROUP = 4
+PAIR = 2
+GROUPS = MASKS // GROUP
+PAIRS_IN_GROUP = GROUP // PAIR
+ROUNDS = GROUPS * ROW_TILES
+PAIRS = MASKS // PAIR
+WORDS = K // 2
+PLANE_MASKS = 8
+PLANE_TILES = MASKS // PLANE_MASKS
+
+FLOPS = 2 * BATCH * MASKS * K * N
+
+
+def tile_paralleldense_e_kernel(tc, x, W_words, W_scales, b, out):
+    nc = tc.nc
+    with ExitStack() as ctx:
+        keep = ctx.enter_context(tc.tile_pool(name="keep", bufs=1))
+        stage = ctx.enter_context(tc.tile_pool(name="stage", bufs=3))
+        results = ctx.enter_context(tc.tile_pool(name="results", bufs=ROUNDS * PAIRS_IN_GROUP))
+        turned_banks = ctx.enter_context(tc.psum_pool(name="turned_banks", bufs=2))
+        bias_banks = ctx.enter_context(tc.psum_pool(name="bias_banks", bufs=2))
+        product_banks = ctx.enter_context(tc.psum_pool(name="product_banks", bufs=4))
+
+        ident_f32 = keep.tile([P, P], F32)
+        make_identity(nc, ident_f32[:])
+        ident_bf16 = keep.tile([P, P], BF16)
+        make_identity(nc, ident_bf16[:])
+
+        w_planes = [
+            keep.tile([P, PLANE_MASKS, N], U8, name="w_planes_%d" % part, align_bytes=64)
+            for part in range(PLANE_TILES)
+        ]
+        b_rows = keep.tile([P, P], BF16)
+        nc.vector.memset(b_rows[:], 0.0)
+        for plane_tile in w_planes:
+            nc.vector.memset(plane_tile[:].bitcast(I32), 0)
+
+        x_rows = x.rearrange("(r p) m k -> r p (m k)", p=P)
+        w_word_rows = W_words.bitcast(I32).rearrange("g p w -> p g w")
+        w_scale_rows = W_scales.bitcast(I32).rearrange("g q w -> q g w")
+        x_tiles = {}
+        w_tiles = {}
+
+        def load_x(group, row_tile):
+            x_tile = keep.tile([P, GROUP * K], BF16, name="x_%d_%d" % (group, row_tile))
+            nc.sync.dma_start(out=x_tile[:], in_=x_rows[row_tile, :, group * GROUP * K : (group + 1) * GROUP * K])
+            x_tiles[(group, row_tile)] = x_tile
+
+        def load_w(group):
+            w_tile = keep.tile([P, GROUP, 2 * N], U8, name="w_%d" % group, align_bytes=64)
+            nc.sync.dma_start(out=w_tile[:].bitcast(I32), in_=w_word_rows[:, group * GROUP : (group + 1) * GROUP, :])
+            w_tiles[group] = w_tile
+
+        load_x(0, 0)
+        nc.sync.dma_start(out=b_rows[0 : MASKS * (N // P), :], in_=b.rearrange("m (c n) -> (m c) n", n=P))
+        for part in range(PLANE_TILES):
+            for q in range(8):
+                first_partition = 32 * (q // 4) + q % 4
+                nc.sync.dma_start(
+                    out=w_planes[part][first_partition:P:64, :, :].bitcast(I32),
+                    in_=w_scale_rows[q:16:8, part * PLANE_MASKS : (part + 1) * PLANE_MASKS, :],
+                )
+        load_w(0)
+        load_x(0, 1)
+        for group in range(1, GROUPS):
+            load_x(group, 0)
+            load_w(group)
+            load_x(group, 1)
+
+        b_cols_bank = bias_banks.tile([P, P], BF16, tag="bias")
+        nc.tensor.transpose(b_cols_bank[:], b_rows[:], ident_bf16[:])
+        b_cols = keep.tile([P, P], BF16)
+        nc.scalar.copy(out=b_cols[:], in_=b_cols_bank[:])
+
+        bias_tiles = {}
+        grouped_tiles = {}
+        x_code_tiles = {}
+        x_plane_tiles = {}
+
+        def broadcast_bias(pair):
+            bank = bias_banks.tile([P, PAIR * N], BF16, tag="bias")
+            chunks = PAIR * N // P
+            for c in range(chunks):
+                column = pair * chunks + c
+                nc.tensor.transpose(
+                    bank[:, c * P : (c + 1) * P], b_cols[:, column : column + 1].to_broadcast([P, P]), ident_bf16[:]
+                )
+            bias_tile = keep.tile([P, PAIR * N], BF16, name="bias_%d" % pair)
+            nc.scalar.copy(out=bias_tile[:], in_=bank[:])
+            bias_tiles[pair] = bias_tile
+
+        def transpose_round(rnd):
+            x_words = x_tiles[divmod(rnd, ROW_TILES)][:].bitcast(F32)
+            grouped = stage.tile([P, GROUP, P, PACK], BF16, align_bytes=64)
+            for half in range(PAIRS_IN_GROUP):
+                turned = turned_banks.tile([P, PAIR, 2, P], F32)
+                for i in range(PAIR):
+                    first_word = (half * PAIR + i) * WORDS
+                    for u in range(2):
+                        nc.tensor.transpose(
+                            turned[:, i, u, :], x_words[:, first_word + u : first_word + WORDS : 2], ident_f32[:]
+                        )
+                nc.scalar.copy(
+                    out=grouped[:, half * PAIR : (half + 1) * PAIR, :, :].bitcast(F32),
+                    in_=turned[:].rearrange("p i u row -> p i row u"),
+                )
+            grouped_tiles[rnd] = grouped
+
+        def quantise_round(rnd):
+            x_codes = stage.tile([P, GROUP * P], U32, align_bytes=64)
+            x_planes = stage.tile([P, GROUP * P], U8, align_bytes=64)
+            nc.vector.quantize_mx(
+                out=x_codes[:].bitcast(FP8X4),
+                scales=x_planes[:],
+                in_=grouped_tiles[rnd][:].rearrange("p i row t -> p (i row t)"),
+            )
+            x_code_tiles[rnd] = x_codes
+            x_plane_tiles[rnd] = x_planes
+
+        def multiply_round(rnd):
+            group, row_tile = divmod(rnd, ROW_TILES)
+            for half in range(PAIRS_IN_GROUP):
+                pair = group * PAIRS_IN_GROUP + half
+                result = results.tile([P, PAIR * N], F32)
+                for i in range(PAIR):
+                    in_group = half * PAIR + i
+                    mask = group * GROUP + in_group
+                    rows = slice(in_group * P, (in_group + 1) * P)
+                    cols = slice(i * N, (i + 1) * N)
+                    product = product_banks.tile([P, N], F32)
+                    nc.tensor.matmul_mx(
+                        out=product[:],
+                        lhsT=x_code_tiles[rnd][:, rows].bitcast(FP8X4),
+                        lhsT_scale=x_plane_tiles[rnd][:, rows],
+                        rhs=w_tiles[group][:, in_group, :].bitcast(FP4X4),
+                        rhs_scale=w_planes[mask // PLANE_MASKS][:, mask % PLANE_MASKS, :],
+                        start=True,
+                        stop=True,
+                    )
+                    nc.vector.tensor_tensor(
+                        out=result[:, cols], in0=product[:], in1=bias_tiles[pair][:, cols], op=mybir.AluOpType.add
+                    )
+                nc.scalar.activation(out=result[:], in_=result[:], func=mybir.ActivationFunctionType.Relu)
+                nc.sync.dma_start(
+                    out=out[row_tile * P : (row_tile + 1) * P, pair * PAIR * N : (pair + 1) * PAIR * N], in_=result[:]
+                )
+
+        assert PAIRS == ROUNDS
+        for step in range(ROUNDS + 2):
+            if step < ROUNDS:
+                broadcast_bias(step)
+                transpose_round(step)
+            if 1 <= step <= ROUNDS:
+                quantise_round(step - 1)
+            if step >= 2:
+                multiply_round(step - 2)

@@ -160,7 +160,17 @@ def tile_paralleldense_e_kernel(tc, x, W_words, W_scales, b, out):
                     nc.vector.tensor_tensor(
                         out=result[:, cols], in0=product[:], in1=bias_tiles[pair][:, cols], op=mybir.AluOpType.add
                     )
-                nc.scalar.activation(out=result[:], in_=result[:], func=mybir.ActivationFunctionType.Relu)
+                if pair % 2 == 0:
+                    nc.scalar.activation(out=result[:], in_=result[:], func=mybir.ActivationFunctionType.Relu)
+                else:
+                    nc.gpsimd.tensor_scalar(
+                        out=result[:],
+                        in0=result[:],
+                        scalar1=float("inf"),
+                        scalar2=0.0,
+                        op0=mybir.AluOpType.min,
+                        op1=mybir.AluOpType.max,
+                    )
                 nc.sync.dma_start(
                     out=out[row_tile * P : (row_tile + 1) * P, pair * PAIR * N : (pair + 1) * PAIR * N], in_=result[:]
                 )

@@ -18,15 +18,12 @@ MASKS = 16
 K = 512
 N = 512
 ROW_TILES = BATCH // P
-GROUP = 4
 PAIR = 2
-GROUPS = MASKS // GROUP
-PAIRS_IN_GROUP = GROUP // PAIR
-ROUNDS = GROUPS * ROW_TILES
-PAIRS = MASKS // PAIR
+ROUNDS = MASKS // PAIR
 WORDS = K // 2
+W_LOAD_MASKS = 4
 PLANE_MASKS = 8
-PLANE_TILES = MASKS // PLANE_MASKS
+BIAS_ROW = 2 * P
 
 FLOPS = 2 * BATCH * MASKS * K * N
 
@@ -36,151 +33,156 @@ def tile_paralleldense_e_kernel(tc, x, W_words, W_scales, b, out):
     with ExitStack() as ctx:
         keep = ctx.enter_context(tc.tile_pool(name="keep", bufs=1))
         stage = ctx.enter_context(tc.tile_pool(name="stage", bufs=3))
-        results = ctx.enter_context(tc.tile_pool(name="results", bufs=ROUNDS * PAIRS_IN_GROUP))
+        results = ctx.enter_context(tc.tile_pool(name="results", bufs=ROUNDS * ROW_TILES))
         turned_banks = ctx.enter_context(tc.psum_pool(name="turned_banks", bufs=2))
-        bias_banks = ctx.enter_context(tc.psum_pool(name="bias_banks", bufs=2))
-        product_banks = ctx.enter_context(tc.psum_pool(name="product_banks", bufs=4))
+        bias_banks = ctx.enter_context(tc.psum_pool(name="bias_banks", bufs=1))
+        product_banks = ctx.enter_context(tc.psum_pool(name="product_banks", bufs=5))
+        ctx.enter_context(tc.manual_schedule())
 
-        ident_f32 = keep.tile([P, P], F32)
-        make_identity(nc, ident_f32[:])
-        ident_bf16 = keep.tile([P, P], BF16)
-        make_identity(nc, ident_bf16[:])
-
+        ident = keep.tile([P, P], F32)
+        make_identity(nc, ident[:])
+        b_rows = keep.tile([P, BIAS_ROW], BF16)
+        nc.vector.memset(b_rows[:], 0.0)
         w_planes = [
             keep.tile([P, PLANE_MASKS, N], U8, name="w_planes_%d" % part, align_bytes=64)
-            for part in range(PLANE_TILES)
+            for part in range(MASKS // PLANE_MASKS)
         ]
-        b_rows = keep.tile([P, P], BF16)
-        nc.vector.memset(b_rows[:], 0.0)
         for plane_tile in w_planes:
             nc.vector.memset(plane_tile[:].bitcast(I32), 0)
 
-        x_rows = x.rearrange("(r p) m k -> r p (m k)", p=P)
+        x_rows = x.rearrange("(r p) m k -> p r (m k)", p=P)
         w_word_rows = W_words.bitcast(I32).rearrange("g p w -> p g w")
         w_scale_rows = W_scales.bitcast(I32).rearrange("g q w -> q g w")
         x_tiles = {}
         w_tiles = {}
 
-        def load_x(group, row_tile):
-            x_tile = keep.tile([P, GROUP * K], BF16, name="x_%d_%d" % (group, row_tile))
-            nc.sync.dma_start(out=x_tile[:], in_=x_rows[row_tile, :, group * GROUP * K : (group + 1) * GROUP * K])
-            x_tiles[(group, row_tile)] = x_tile
+        def load_x(rnd):
+            x_tile = keep.tile([P, ROW_TILES, PAIR * K], BF16, name="x_%d" % rnd)
+            nc.sync.dma_start(out=x_tile[:], in_=x_rows[:, :, rnd * PAIR * K : (rnd + 1) * PAIR * K])
+            x_tiles[rnd] = x_tile
 
         def load_w(group):
-            w_tile = keep.tile([P, GROUP, 2 * N], U8, name="w_%d" % group, align_bytes=64)
-            nc.sync.dma_start(out=w_tile[:].bitcast(I32), in_=w_word_rows[:, group * GROUP : (group + 1) * GROUP, :])
+            w_tile = keep.tile([P, W_LOAD_MASKS, 2 * N], U8, name="w_%d" % group, align_bytes=64)
+            mask_range = slice(group * W_LOAD_MASKS, (group + 1) * W_LOAD_MASKS)
+            nc.sync.dma_start(out=w_tile[:].bitcast(I32), in_=w_word_rows[:, mask_range, :])
             w_tiles[group] = w_tile
 
-        load_x(0, 0)
-        nc.sync.dma_start(out=b_rows[0 : MASKS * (N // P), :], in_=b.rearrange("m (c n) -> (m c) n", n=P))
-        for part in range(PLANE_TILES):
-            for q in range(8):
-                first_partition = 32 * (q // 4) + q % 4
-                nc.sync.dma_start(
-                    out=w_planes[part][first_partition:P:64, :, :].bitcast(I32),
-                    in_=w_scale_rows[q:16:8, part * PLANE_MASKS : (part + 1) * PLANE_MASKS, :],
-                )
-        load_w(0)
-        load_x(0, 1)
-        for group in range(1, GROUPS):
-            load_x(group, 0)
-            load_w(group)
-            load_x(group, 1)
+        def load_planes(part):
+            mask_range = slice(part * PLANE_MASKS, (part + 1) * PLANE_MASKS)
+            for j in range(4):
+                nc.sync.dma_start(out=w_planes[part][j:P:32, :, :].bitcast(I32), in_=w_scale_rows[j:16:4, mask_range, :])
 
-        b_cols_bank = bias_banks.tile([P, P], BF16, tag="bias")
-        nc.tensor.transpose(b_cols_bank[:], b_rows[:], ident_bf16[:])
-        b_cols = keep.tile([P, P], BF16)
+        nc.sync.dma_start(out=b_rows[0 : MASKS * N // BIAS_ROW, :], in_=b.rearrange("m (c n) -> (m c) n", n=BIAS_ROW))
+        load_x(0)
+        load_x(1)
+        load_planes(0)
+        load_w(0)
+        load_x(2)
+        load_x(3)
+        load_w(1)
+        load_planes(1)
+        load_x(4)
+        load_x(5)
+        load_w(2)
+        load_x(6)
+        load_x(7)
+        load_w(3)
+
+        b_cols_bank = bias_banks.tile([P, P], F32, tag="bias")
+        nc.tensor.transpose(b_cols_bank[:], b_rows[:].bitcast(F32), ident[:])
+        b_cols = keep.tile([P, P], F32)
         nc.scalar.copy(out=b_cols[:], in_=b_cols_bank[:])
 
         bias_tiles = {}
         grouped_tiles = {}
         x_code_tiles = {}
         x_plane_tiles = {}
+        result_tiles = {}
 
-        def broadcast_bias(pair):
-            bank = bias_banks.tile([P, PAIR * N], BF16, tag="bias")
-            chunks = PAIR * N // P
-            for c in range(chunks):
-                column = pair * chunks + c
+        def broadcast_bias(rnd):
+            bank = bias_banks.tile([P, PAIR * N // 2], F32, tag="bias")
+            for c in range(PAIR * N // BIAS_ROW):
+                column = rnd * (PAIR * N // BIAS_ROW) + c
                 nc.tensor.transpose(
-                    bank[:, c * P : (c + 1) * P], b_cols[:, column : column + 1].to_broadcast([P, P]), ident_bf16[:]
+                    bank[:, c * P : (c + 1) * P], b_cols[:, column : column + 1].to_broadcast([P, P]), ident[:]
                 )
-            bias_tile = keep.tile([P, PAIR * N], BF16, name="bias_%d" % pair)
+            bias_tile = keep.tile([P, PAIR * N // 2], F32, name="bias_%d" % rnd)
             nc.scalar.copy(out=bias_tile[:], in_=bank[:])
-            bias_tiles[pair] = bias_tile
+            bias_tiles[rnd] = bias_tile
 
         def transpose_round(rnd):
-            x_words = x_tiles[divmod(rnd, ROW_TILES)][:].bitcast(F32)
-            grouped = stage.tile([P, GROUP, P, PACK], BF16, align_bytes=64)
-            for half in range(PAIRS_IN_GROUP):
+            x_words = x_tiles[rnd][:].bitcast(F32)
+            grouped = stage.tile([P, ROW_TILES, PAIR, P, PACK], BF16, align_bytes=64)
+            for r in range(ROW_TILES):
                 turned = turned_banks.tile([P, PAIR, 2, P], F32)
                 for i in range(PAIR):
-                    first_word = (half * PAIR + i) * WORDS
                     for u in range(2):
                         nc.tensor.transpose(
-                            turned[:, i, u, :], x_words[:, first_word + u : first_word + WORDS : 2], ident_f32[:]
+                            turned[:, i, u, :], x_words[:, r, i * WORDS + u : (i + 1) * WORDS : 2], ident[:]
                         )
                 nc.scalar.copy(
-                    out=grouped[:, half * PAIR : (half + 1) * PAIR, :, :].bitcast(F32),
-                    in_=turned[:].rearrange("p i u row -> p i row u"),
+                    out=grouped[:, r, :, :, :].bitcast(F32), in_=turned[:].rearrange("p i u row -> p i row u")
                 )
             grouped_tiles[rnd] = grouped
 
         def quantise_round(rnd):
-            x_codes = stage.tile([P, GROUP * P], U32, align_bytes=64)
-            x_planes = stage.tile([P, GROUP * P], U8, align_bytes=64)
+            x_codes = stage.tile([P, ROW_TILES * PAIR * P], U32, align_bytes=64)
+            x_planes = stage.tile([P, ROW_TILES * PAIR * P], U8, align_bytes=64)
             nc.vector.quantize_mx(
                 out=x_codes[:].bitcast(FP8X4),
                 scales=x_planes[:],
-                in_=grouped_tiles[rnd][:].rearrange("p i row t -> p (i row t)"),
+                in_=grouped_tiles[rnd][:].rearrange("p r i row t -> p (r i row t)"),
             )
             x_code_tiles[rnd] = x_codes
             x_plane_tiles[rnd] = x_planes
 
         def multiply_round(rnd):
-            group, row_tile = divmod(rnd, ROW_TILES)
-            for half in range(PAIRS_IN_GROUP):
-                pair = group * PAIRS_IN_GROUP + half
+            bias = bias_tiles[rnd][:].bitcast(BF16)
+            for r in range(ROW_TILES):
                 result = results.tile([P, PAIR * N], F32)
                 for i in range(PAIR):
-                    in_group = half * PAIR + i
-                    mask = group * GROUP + in_group
-                    rows = slice(in_group * P, (in_group + 1) * P)
+                    mask = rnd * PAIR + i
+                    rows = slice((r * PAIR + i) * P, (r * PAIR + i + 1) * P)
                     cols = slice(i * N, (i + 1) * N)
                     product = product_banks.tile([P, N], F32)
                     nc.tensor.matmul_mx(
                         out=product[:],
                         lhsT=x_code_tiles[rnd][:, rows].bitcast(FP8X4),
                         lhsT_scale=x_plane_tiles[rnd][:, rows],
-                        rhs=w_tiles[group][:, in_group, :].bitcast(FP4X4),
+                        rhs=w_tiles[mask // W_LOAD_MASKS][:, mask % W_LOAD_MASKS, :].bitcast(FP4X4),
                         rhs_scale=w_planes[mask // PLANE_MASKS][:, mask % PLANE_MASKS, :],
                         start=True,
                         stop=True,
                     )
                     nc.vector.tensor_tensor(
-                        out=result[:, cols], in0=product[:], in1=bias_tiles[pair][:, cols], op=mybir.AluOpType.add
+                        out=result[:, cols], in0=product[:], in1=bias[:, cols], op=mybir.AluOpType.add
                     )
-                if pair % 2 == 0:
-                    nc.scalar.activation(out=result[:], in_=result[:], func=mybir.ActivationFunctionType.Relu)
-                else:
-                    nc.gpsimd.tensor_scalar(
-                        out=result[:],
-                        in0=result[:],
-                        scalar1=float("inf"),
-                        scalar2=0.0,
-                        op0=mybir.AluOpType.min,
-                        op1=mybir.AluOpType.max,
-                    )
+                result_tiles[(rnd, r)] = result
+
+        def finish_round(rnd):
+            first, second = result_tiles[(rnd, 0)], result_tiles[(rnd, 1)]
+            nc.gpsimd.tensor_scalar(
+                out=first[:],
+                in0=first[:],
+                scalar1=float("inf"),
+                scalar2=0.0,
+                op0=mybir.AluOpType.min,
+                op1=mybir.AluOpType.max,
+            )
+            nc.scalar.activation(out=second[:], in_=second[:], func=mybir.ActivationFunctionType.Relu)
+            for r in range(ROW_TILES):
                 nc.sync.dma_start(
-                    out=out[row_tile * P : (row_tile + 1) * P, pair * PAIR * N : (pair + 1) * PAIR * N], in_=result[:]
+                    out=out[r * P : (r + 1) * P, rnd * PAIR * N : (rnd + 1) * PAIR * N], in_=result_tiles[(rnd, r)][:]
                 )
 
-        assert PAIRS == ROUNDS
         for step in range(ROUNDS + 2):
             if step < ROUNDS:
-                broadcast_bias(step)
                 transpose_round(step)
-            if 1 <= step <= ROUNDS:
-                quantise_round(step - 1)
             if step >= 2:
-                multiply_round(step - 2)
+                finish_round(step - 2)
+            if step < ROUNDS:
+                quantise_round(step)
+            if 1 <= step <= ROUNDS:
+                multiply_round(step - 1)
+            if step < ROUNDS:
+                broadcast_bias(step)

@@ -136,53 +136,59 @@ def tile_paralleldense_e_kernel(tc, x, W_words, W_scales, b, out):
             x_code_tiles[rnd] = x_codes
             x_plane_tiles[rnd] = x_planes
 
-        def multiply_round(rnd):
+        def multiply_row_tile(rnd, r):
             bias = bias_tiles[rnd][:].bitcast(BF16)
-            for r in range(ROW_TILES):
-                result = results.tile([P, PAIR * N], F32)
-                for i in range(PAIR):
-                    mask = rnd * PAIR + i
-                    rows = slice((r * PAIR + i) * P, (r * PAIR + i + 1) * P)
-                    cols = slice(i * N, (i + 1) * N)
-                    product = product_banks.tile([P, N], F32)
-                    nc.tensor.matmul_mx(
-                        out=product[:],
-                        lhsT=x_code_tiles[rnd][:, rows].bitcast(FP8X4),
-                        lhsT_scale=x_plane_tiles[rnd][:, rows],
-                        rhs=w_tiles[mask // W_LOAD_MASKS][:, mask % W_LOAD_MASKS, :].bitcast(FP4X4),
-                        rhs_scale=w_planes[mask // PLANE_MASKS][:, mask % PLANE_MASKS, :],
-                        start=True,
-                        stop=True,
-                    )
-                    nc.vector.tensor_tensor(
-                        out=result[:, cols], in0=product[:], in1=bias[:, cols], op=mybir.AluOpType.add
-                    )
-                result_tiles[(rnd, r)] = result
-
-        def finish_round(rnd):
-            first, second = result_tiles[(rnd, 0)], result_tiles[(rnd, 1)]
-            nc.gpsimd.tensor_scalar(
-                out=first[:],
-                in0=first[:],
-                scalar1=float("inf"),
-                scalar2=0.0,
-                op0=mybir.AluOpType.min,
-                op1=mybir.AluOpType.max,
-            )
-            nc.scalar.activation(out=second[:], in_=second[:], func=mybir.ActivationFunctionType.Relu)
-            for r in range(ROW_TILES):
-                nc.sync.dma_start(
-                    out=out[r * P : (r + 1) * P, rnd * PAIR * N : (rnd + 1) * PAIR * N], in_=result_tiles[(rnd, r)][:]
+            result = results.tile([P, PAIR * N], F32)
+            for i in range(PAIR):
+                mask = rnd * PAIR + i
+                rows = slice((r * PAIR + i) * P, (r * PAIR + i + 1) * P)
+                cols = slice(i * N, (i + 1) * N)
+                product = product_banks.tile([P, N], F32)
+                nc.tensor.matmul_mx(
+                    out=product[:],
+                    lhsT=x_code_tiles[rnd][:, rows].bitcast(FP8X4),
+                    lhsT_scale=x_plane_tiles[rnd][:, rows],
+                    rhs=w_tiles[mask // W_LOAD_MASKS][:, mask % W_LOAD_MASKS, :].bitcast(FP4X4),
+                    rhs_scale=w_planes[mask // PLANE_MASKS][:, mask % PLANE_MASKS, :],
+                    start=True,
+                    stop=True,
                 )
+                nc.vector.tensor_tensor(out=result[:, cols], in0=product[:], in1=bias[:, cols], op=mybir.AluOpType.add)
+            result_tiles[(rnd, r)] = result
+
+        def finish_round(rnd, pieces):
+            width = PAIR * N // pieces
+            for r in range(ROW_TILES):
+                for piece in range(pieces):
+                    part_of_result = result_tiles[(rnd, r)][:, piece * width : (piece + 1) * width]
+                    if r == 0:
+                        nc.gpsimd.tensor_scalar(
+                            out=part_of_result,
+                            in0=part_of_result,
+                            scalar1=float("inf"),
+                            scalar2=0.0,
+                            op0=mybir.AluOpType.min,
+                            op1=mybir.AluOpType.max,
+                        )
+                    else:
+                        nc.scalar.activation(
+                            out=part_of_result, in_=part_of_result, func=mybir.ActivationFunctionType.Relu
+                        )
+                    first_col = rnd * PAIR * N + piece * width
+                    nc.sync.dma_start(
+                        out=out[r * P : (r + 1) * P, first_col : first_col + width], in_=part_of_result
+                    )
 
         for step in range(ROUNDS + 2):
             if step < ROUNDS:
                 transpose_round(step)
             if step >= 2:
-                finish_round(step - 2)
+                finish_round(step - 2, pieces=PAIR if step - 2 == ROUNDS - 1 else 1)
+            if 1 <= step <= ROUNDS:
+                multiply_row_tile(step - 1, 0)
             if step < ROUNDS:
                 quantise_round(step)
             if 1 <= step <= ROUNDS:
-                multiply_round(step - 1)
+                multiply_row_tile(step - 1, 1)
             if step < ROUNDS:
                 broadcast_bias(step)

@@ -18,10 +18,12 @@ MASKS = 16
 K = 512
 N = 512
 ROW_TILES = BATCH // P
+GROUP = 4
 PAIR = 2
-ROUNDS = MASKS // PAIR
+PAIRS_IN_GROUP = GROUP // PAIR
+PAIRS = MASKS // PAIR
+ROUNDS = (MASKS // GROUP) * ROW_TILES
 WORDS = K // 2
-W_LOAD_MASKS = 4
 PLANE_MASKS = 8
 BIAS_ROW = 2 * P
 
@@ -33,7 +35,7 @@ def tile_paralleldense_e_kernel(tc, x, W_words, W_scales, b, out):
     with ExitStack() as ctx:
         keep = ctx.enter_context(tc.tile_pool(name="keep", bufs=1))
         stage = ctx.enter_context(tc.tile_pool(name="stage", bufs=3))
-        results = ctx.enter_context(tc.tile_pool(name="results", bufs=ROUNDS * ROW_TILES))
+        results = ctx.enter_context(tc.tile_pool(name="results", bufs=ROUNDS))
         turned_banks = ctx.enter_context(tc.psum_pool(name="turned_banks", bufs=2))
         bias_banks = ctx.enter_context(tc.psum_pool(name="bias_banks", bufs=1))
         product_banks = ctx.enter_context(tc.psum_pool(name="product_banks", bufs=5))
@@ -50,21 +52,21 @@ def tile_paralleldense_e_kernel(tc, x, W_words, W_scales, b, out):
         for plane_tile in w_planes:
             nc.vector.memset(plane_tile[:].bitcast(I32), 0)
 
-        x_rows = x.rearrange("(r p) m k -> p r (m k)", p=P)
+        x_rows = x.rearrange("(r p) m k -> r p (m k)", p=P)
         w_word_rows = W_words.bitcast(I32).rearrange("g p w -> p g w")
         w_scale_rows = W_scales.bitcast(I32).rearrange("g q w -> q g w")
         x_tiles = {}
         w_tiles = {}
 
         def load_x(rnd):
-            x_tile = keep.tile([P, ROW_TILES, PAIR * K], BF16, name="x_%d" % rnd)
-            nc.sync.dma_start(out=x_tile[:], in_=x_rows[:, :, rnd * PAIR * K : (rnd + 1) * PAIR * K])
+            group, r = divmod(rnd, ROW_TILES)
+            x_tile = keep.tile([P, GROUP * K], BF16, name="x_%d" % rnd)
+            nc.sync.dma_start(out=x_tile[:], in_=x_rows[r, :, group * GROUP * K : (group + 1) * GROUP * K])
             x_tiles[rnd] = x_tile
 
         def load_w(group):
-            w_tile = keep.tile([P, W_LOAD_MASKS, 2 * N], U8, name="w_%d" % group, align_bytes=64)
-            mask_range = slice(group * W_LOAD_MASKS, (group + 1) * W_LOAD_MASKS)
-            nc.sync.dma_start(out=w_tile[:].bitcast(I32), in_=w_word_rows[:, mask_range, :])
+            w_tile = keep.tile([P, GROUP, 2 * N], U8, name="w_%d" % group, align_bytes=64)
+            nc.sync.dma_start(out=w_tile[:].bitcast(I32), in_=w_word_rows[:, group * GROUP : (group + 1) * GROUP, :])
             w_tiles[group] = w_tile
 
         def load_planes(part):
@@ -78,15 +80,15 @@ def tile_paralleldense_e_kernel(tc, x, W_words, W_scales, b, out):
         load_planes(0)
         load_w(0)
         load_x(2)
-        load_x(3)
         load_w(1)
+        load_x(3)
         load_planes(1)
         load_x(4)
-        load_x(5)
         load_w(2)
+        load_x(5)
         load_x(6)
-        load_x(7)
         load_w(3)
+        load_x(7)
 
         b_cols_bank = bias_banks.tile([P, P], F32, tag="bias")
         nc.tensor.transpose(b_cols_bank[:], b_rows[:].bitcast(F32), ident[:])
@@ -99,96 +101,108 @@ def tile_paralleldense_e_kernel(tc, x, W_words, W_scales, b, out):
         x_plane_tiles = {}
         result_tiles = {}
 
-        def broadcast_bias(rnd):
+        def broadcast_bias(pair):
             bank = bias_banks.tile([P, PAIR * N // 2], F32, tag="bias")
             for c in range(PAIR * N // BIAS_ROW):
-                column = rnd * (PAIR * N // BIAS_ROW) + c
+                column = pair * (PAIR * N // BIAS_ROW) + c
                 nc.tensor.transpose(
                     bank[:, c * P : (c + 1) * P], b_cols[:, column : column + 1].to_broadcast([P, P]), ident[:]
                 )
-            bias_tile = keep.tile([P, PAIR * N // 2], F32, name="bias_%d" % rnd)
+            bias_tile = keep.tile([P, PAIR * N // 2], F32, name="bias_%d" % pair)
             nc.scalar.copy(out=bias_tile[:], in_=bank[:])
-            bias_tiles[rnd] = bias_tile
+            bias_tiles[pair] = bias_tile
 
         def transpose_round(rnd):
             x_words = x_tiles[rnd][:].bitcast(F32)
-            grouped = stage.tile([P, ROW_TILES, PAIR, P, PACK], BF16, align_bytes=64)
-            for r in range(ROW_TILES):
+            grouped = stage.tile([P, GROUP, P, PACK], BF16, align_bytes=64)
+            for half in range(PAIRS_IN_GROUP):
                 turned = turned_banks.tile([P, PAIR, 2, P], F32)
                 for i in range(PAIR):
+                    first_word = (half * PAIR + i) * WORDS
                     for u in range(2):
                         nc.tensor.transpose(
-                            turned[:, i, u, :], x_words[:, r, i * WORDS + u : (i + 1) * WORDS : 2], ident[:]
+                            turned[:, i, u, :], x_words[:, first_word + u : first_word + WORDS : 2], ident[:]
                         )
                 nc.scalar.copy(
-                    out=grouped[:, r, :, :, :].bitcast(F32), in_=turned[:].rearrange("p i u row -> p i row u")
+                    out=grouped[:, half * PAIR : (half + 1) * PAIR, :, :].bitcast(F32),
+                    in_=turned[:].rearrange("p i u row -> p i row u"),
                 )
             grouped_tiles[rnd] = grouped
 
         def quantise_round(rnd):
-            x_codes = stage.tile([P, ROW_TILES * PAIR * P], U32, align_bytes=64)
-            x_planes = stage.tile([P, ROW_TILES * PAIR * P], U8, align_bytes=64)
+            x_codes = stage.tile([P, GROUP * P], U32, align_bytes=64)
+            x_planes = stage.tile([P, GROUP * P], U8, align_bytes=64)
             nc.vector.quantize_mx(
                 out=x_codes[:].bitcast(FP8X4),
                 scales=x_planes[:],
-                in_=grouped_tiles[rnd][:].rearrange("p r i row t -> p (r i row t)"),
+                in_=grouped_tiles[rnd][:].rearrange("p i row t -> p (i row t)"),
             )
             x_code_tiles[rnd] = x_codes
             x_plane_tiles[rnd] = x_planes
 
-        def multiply_row_tile(rnd, r):
-            bias = bias_tiles[rnd][:].bitcast(BF16)
-            result = results.tile([P, PAIR * N], F32)
+        def multiply_pair(rnd, half):
+            group = rnd // ROW_TILES
+            bias = bias_tiles[group * PAIRS_IN_GROUP + half][:].bitcast(BF16)
+            if half == 0:
+                result_tiles[rnd] = results.tile([P, GROUP * N], F32, name="result")
             for i in range(PAIR):
-                mask = rnd * PAIR + i
-                rows = slice((r * PAIR + i) * P, (r * PAIR + i + 1) * P)
-                cols = slice(i * N, (i + 1) * N)
+                in_group = half * PAIR + i
+                mask = group * GROUP + in_group
+                rows = slice(in_group * P, (in_group + 1) * P)
                 product = product_banks.tile([P, N], F32)
                 nc.tensor.matmul_mx(
                     out=product[:],
                     lhsT=x_code_tiles[rnd][:, rows].bitcast(FP8X4),
                     lhsT_scale=x_plane_tiles[rnd][:, rows],
-                    rhs=w_tiles[mask // W_LOAD_MASKS][:, mask % W_LOAD_MASKS, :].bitcast(FP4X4),
+                    rhs=w_tiles[group][:, in_group, :].bitcast(FP4X4),
                     rhs_scale=w_planes[mask // PLANE_MASKS][:, mask % PLANE_MASKS, :],
                     start=True,
                     stop=True,
                 )
-                nc.vector.tensor_tensor(out=result[:, cols], in0=product[:], in1=bias[:, cols], op=mybir.AluOpType.add)
-            result_tiles[(rnd, r)] = result
+                nc.vector.tensor_tensor(
+                    out=result_tiles[rnd][:, in_group * N : (in_group + 1) * N],
+                    in0=product[:],
+                    in1=bias[:, i * N : (i + 1) * N],
+                    op=mybir.AluOpType.add,
+                )
 
-        def finish_round(rnd, pieces):
-            width = PAIR * N // pieces
-            for r in range(ROW_TILES):
-                for piece in range(pieces):
-                    part_of_result = result_tiles[(rnd, r)][:, piece * width : (piece + 1) * width]
-                    if r == 0:
-                        nc.gpsimd.tensor_scalar(
-                            out=part_of_result,
-                            in0=part_of_result,
-                            scalar1=float("inf"),
-                            scalar2=0.0,
-                            op0=mybir.AluOpType.min,
-                            op1=mybir.AluOpType.max,
-                        )
-                    else:
-                        nc.scalar.activation(
-                            out=part_of_result, in_=part_of_result, func=mybir.ActivationFunctionType.Relu
-                        )
-                    first_col = rnd * PAIR * N + piece * width
-                    nc.sync.dma_start(
-                        out=out[r * P : (r + 1) * P, first_col : first_col + width], in_=part_of_result
+        def finish_round(rnd, stores):
+            group, r = divmod(rnd, ROW_TILES)
+            relus = max(stores, PAIRS_IN_GROUP)
+            relu_width = GROUP * N // relus
+            for piece in range(relus):
+                values = result_tiles[rnd][:, piece * relu_width : (piece + 1) * relu_width]
+                if piece * relu_width < PAIR * N:
+                    nc.gpsimd.tensor_scalar(
+                        out=values,
+                        in0=values,
+                        scalar1=float("inf"),
+                        scalar2=0.0,
+                        op0=mybir.AluOpType.min,
+                        op1=mybir.AluOpType.max,
                     )
+                else:
+                    nc.scalar.activation(out=values, in_=values, func=mybir.ActivationFunctionType.Relu)
+            store_width = GROUP * N // stores
+            for piece in range(stores):
+                cols = slice(piece * store_width, (piece + 1) * store_width)
+                first_col = group * GROUP * N + piece * store_width
+                nc.sync.dma_start(
+                    out=out[r * P : (r + 1) * P, first_col : first_col + store_width], in_=result_tiles[rnd][:, cols]
+                )
 
+        assert PAIRS == ROUNDS
+        broadcast_bias(0)
         for step in range(ROUNDS + 2):
             if step < ROUNDS:
                 transpose_round(step)
             if step >= 2:
-                finish_round(step - 2, pieces=PAIR if step - 2 == ROUNDS - 1 else 1)
+                finish_round(step - 2, stores=GROUP if step - 2 == ROUNDS - 1 else 1)
             if 1 <= step <= ROUNDS:
-                multiply_row_tile(step - 1, 0)
+                multiply_pair(step - 1, 0)
             if step < ROUNDS:
                 quantise_round(step)
             if 1 <= step <= ROUNDS:
-                multiply_row_tile(step - 1, 1)
-            if step < ROUNDS:
-                broadcast_bias(step)
+                multiply_pair(step - 1, 1)
+            if step + 1 < PAIRS:
+                broadcast_bias(step + 1)

@@ -74,8 +74,8 @@ def tile_paralleldense_e_kernel(tc, x, W_words, W_scales, b, out):
             for j in range(4):
                 nc.sync.dma_start(out=w_planes[part][j:P:32, :, :].bitcast(I32), in_=w_scale_rows[j:16:4, mask_range, :])
 
-        nc.sync.dma_start(out=b_rows[0 : MASKS * N // BIAS_ROW, :], in_=b.rearrange("m (c n) -> (m c) n", n=BIAS_ROW))
         load_x(0)
+        nc.sync.dma_start(out=b_rows[0 : MASKS * N // BIAS_ROW, :], in_=b.rearrange("m (c n) -> (m c) n", n=BIAS_ROW))
         load_x(1)
         load_planes(0)
         load_w(0)
@@ -90,10 +90,12 @@ def tile_paralleldense_e_kernel(tc, x, W_words, W_scales, b, out):
         load_w(3)
         load_x(7)
 
-        b_cols_bank = bias_banks.tile([P, P], F32, tag="bias")
-        nc.tensor.transpose(b_cols_bank[:], b_rows[:].bitcast(F32), ident[:])
         b_cols = keep.tile([P, P], F32)
-        nc.scalar.copy(out=b_cols[:], in_=b_cols_bank[:])
+
+        def turn_bias():
+            b_cols_bank = bias_banks.tile([P, P], F32, tag="bias")
+            nc.tensor.transpose(b_cols_bank[:], b_rows[:].bitcast(F32), ident[:])
+            nc.scalar.copy(out=b_cols[:], in_=b_cols_bank[:])
 
         bias_tiles = {}
         grouped_tiles = {}
@@ -192,10 +194,12 @@ def tile_paralleldense_e_kernel(tc, x, W_words, W_scales, b, out):
                 )
 
         assert PAIRS == ROUNDS
-        broadcast_bias(0)
         for step in range(ROUNDS + 2):
             if step < ROUNDS:
                 transpose_round(step)
+            if step == 0:
+                turn_bias()
+                broadcast_bias(0)
             if step >= 2:
                 finish_round(step - 2, stores=GROUP if step - 2 == ROUNDS - 1 else 1)
             if 1 <= step <= ROUNDS:

@@ -44,7 +44,8 @@ def tile_paralleldense_e_kernel(tc, x, W_words, W_scales, b, out):
         ident = keep.tile([P, P], F32)
         make_identity(nc, ident[:])
         b_rows = keep.tile([P, BIAS_ROW], BF16)
-        nc.vector.memset(b_rows[:], 0.0)
+        nc.vector.memset(b_rows[32:64, :], 0.0)
+        nc.vector.memset(b_rows[64:P, :], 0.0)
         w_planes = [
             keep.tile([P, PLANE_MASKS, N], U8, name="w_planes_%d" % part, align_bytes=64)
             for part in range(MASKS // PLANE_MASKS)
@@ -74,8 +75,8 @@ def tile_paralleldense_e_kernel(tc, x, W_words, W_scales, b, out):
             for j in range(4):
                 nc.sync.dma_start(out=w_planes[part][j:P:32, :, :].bitcast(I32), in_=w_scale_rows[j:16:4, mask_range, :])
 
+        nc.scalar.dma_start(out=b_rows[0 : MASKS * N // BIAS_ROW, :], in_=b.rearrange("m (c n) -> (m c) n", n=BIAS_ROW))
         load_x(0)
-        nc.sync.dma_start(out=b_rows[0 : MASKS * N // BIAS_ROW, :], in_=b.rearrange("m (c n) -> (m c) n", n=BIAS_ROW))
         load_x(1)
         load_planes(0)
         load_w(0)
@@ -194,12 +195,11 @@ def tile_paralleldense_e_kernel(tc, x, W_words, W_scales, b, out):
                 )
 
         assert PAIRS == ROUNDS
+        turn_bias()
+        broadcast_bias(0)
         for step in range(ROUNDS + 2):
             if step < ROUNDS:
                 transpose_round(step)
-            if step == 0:
-                turn_bias()
-                broadcast_bias(0)
             if step >= 2:
                 finish_round(step - 2, stores=GROUP if step - 2 == ROUNDS - 1 else 1)
             if 1 <= step <= ROUNDS:

@@ -26,6 +26,7 @@ ROUNDS = (MASKS // GROUP) * ROW_TILES
 WORDS = K // 2
 PLANE_MASKS = 8
 BIAS_ROW = 2 * P
+WARM_UP_MATMULS = 5
 
 FLOPS = 2 * BATCH * MASKS * K * N
 
@@ -40,6 +41,12 @@ def tile_paralleldense_e_kernel(tc, x, W_words, W_scales, b, out):
         bias_banks = ctx.enter_context(tc.psum_pool(name="bias_banks", bufs=1))
         product_banks = ctx.enter_context(tc.psum_pool(name="product_banks", bufs=5))
         ctx.enter_context(tc.manual_schedule())
+
+        zeros = keep.tile([P, N], BF16)
+        nc.vector.memset(zeros[:], 0.0)
+        for warm_up in range(WARM_UP_MATMULS):
+            unread = product_banks.tile([P, N], F32, name="product")
+            nc.tensor.matmul(out=unread[:], lhsT=zeros[:, 0:P], rhs=zeros[:], start=True, stop=True)
 
         ident = keep.tile([P, P], F32)
         make_identity(nc, ident[:])
@@ -206,7 +213,7 @@ def tile_paralleldense_e_kernel(tc, x, W_words, W_scales, b, out):
                 multiply_pair(step - 1, 0)
             if step < ROUNDS:
                 quantise_round(step)
-            if 1 <= step <= ROUNDS:
-                multiply_pair(step - 1, 1)
             if step + 1 < PAIRS:
                 broadcast_bias(step + 1)
+            if 1 <= step <= ROUNDS:
+                multiply_pair(step - 1, 1)

from contextlib import ExitStack

import concourse.mybir as mybir
from concourse.masks import make_identity

F32 = mybir.dt.float32
BF16 = mybir.dt.bfloat16
I32 = mybir.dt.int32
U32 = mybir.dt.uint32
U8 = mybir.dt.uint8
FP8X4 = mybir.dt.float8_e4m3fn_x4
FP4X4 = mybir.dt.float4_e2m1fn_x4

P = 128
PACK = 4
BATCH = 256
MASKS = 16
K = 512
N = 512
ROW_TILES = BATCH // P
GROUP = 4
PAIR = 2
PAIRS_IN_GROUP = GROUP // PAIR
PAIRS = MASKS // PAIR
ROUNDS = (MASKS // GROUP) * ROW_TILES
WORDS = K // 2
PLANE_MASKS = 8
BIAS_ROW = 2 * P
WARM_UP_MATMULS = 5

FLOPS = 2 * BATCH * MASKS * K * N


def tile_paralleldense_e_kernel(tc, x, W_words, W_scales, b, out):
    nc = tc.nc
    with ExitStack() as ctx:
        keep = ctx.enter_context(tc.tile_pool(name="keep", bufs=1))
        stage = ctx.enter_context(tc.tile_pool(name="stage", bufs=3))
        results = ctx.enter_context(tc.tile_pool(name="results", bufs=ROUNDS))
        turned_banks = ctx.enter_context(tc.psum_pool(name="turned_banks", bufs=2))
        bias_banks = ctx.enter_context(tc.psum_pool(name="bias_banks", bufs=1))
        product_banks = ctx.enter_context(tc.psum_pool(name="product_banks", bufs=5))
        ctx.enter_context(tc.manual_schedule())

        zeros = keep.tile([P, N], BF16)
        nc.vector.memset(zeros[:], 0.0)
        for warm_up in range(WARM_UP_MATMULS):
            unread = product_banks.tile([P, N], F32, name="product")
            nc.tensor.matmul(out=unread[:], lhsT=zeros[:, 0:P], rhs=zeros[:], start=True, stop=True)

        ident = keep.tile([P, P], F32)
        make_identity(nc, ident[:])
        b_rows = keep.tile([P, BIAS_ROW], BF16)
        nc.vector.memset(b_rows[32:64, :], 0.0)
        nc.vector.memset(b_rows[64:P, :], 0.0)
        w_planes = [
            keep.tile([P, PLANE_MASKS, N], U8, name="w_planes_%d" % part, align_bytes=64)
            for part in range(MASKS // PLANE_MASKS)
        ]
        for plane_tile in w_planes:
            nc.vector.memset(plane_tile[:].bitcast(I32), 0)

        x_rows = x.rearrange("(r p) m k -> r p (m k)", p=P)
        w_word_rows = W_words.bitcast(I32).rearrange("g p w -> p g w")
        w_scale_rows = W_scales.bitcast(I32).rearrange("g q w -> q g w")
        x_tiles = {}
        w_tiles = {}

        def load_x(rnd):
            group, r = divmod(rnd, ROW_TILES)
            x_tile = keep.tile([P, GROUP * K], BF16, name="x_%d" % rnd)
            nc.sync.dma_start(out=x_tile[:], in_=x_rows[r, :, group * GROUP * K : (group + 1) * GROUP * K])
            x_tiles[rnd] = x_tile

        def load_w(group):
            w_tile = keep.tile([P, GROUP, 2 * N], U8, name="w_%d" % group, align_bytes=64)
            nc.sync.dma_start(out=w_tile[:].bitcast(I32), in_=w_word_rows[:, group * GROUP : (group + 1) * GROUP, :])
            w_tiles[group] = w_tile

        def load_planes(part):
            mask_range = slice(part * PLANE_MASKS, (part + 1) * PLANE_MASKS)
            for j in range(4):
                nc.sync.dma_start(out=w_planes[part][j:P:32, :, :].bitcast(I32), in_=w_scale_rows[j:16:4, mask_range, :])

        nc.scalar.dma_start(out=b_rows[0 : MASKS * N // BIAS_ROW, :], in_=b.rearrange("m (c n) -> (m c) n", n=BIAS_ROW))
        load_x(0)
        load_x(1)
        load_planes(0)
        load_w(0)
        load_x(2)
        load_w(1)
        load_x(3)
        load_planes(1)
        load_x(4)
        load_w(2)
        load_x(5)
        load_x(6)
        load_w(3)
        load_x(7)

        b_cols = keep.tile([P, P], F32)

        def turn_bias():
            b_cols_bank = bias_banks.tile([P, P], F32, tag="bias")
            nc.tensor.transpose(b_cols_bank[:], b_rows[:].bitcast(F32), ident[:])
            nc.scalar.copy(out=b_cols[:], in_=b_cols_bank[:])

        bias_tiles = {}
        grouped_tiles = {}
        x_code_tiles = {}
        x_plane_tiles = {}
        result_tiles = {}

        def broadcast_bias(pair):
            bank = bias_banks.tile([P, PAIR * N // 2], F32, tag="bias")
            for c in range(PAIR * N // BIAS_ROW):
                column = pair * (PAIR * N // BIAS_ROW) + c
                nc.tensor.transpose(
                    bank[:, c * P : (c + 1) * P], b_cols[:, column : column + 1].to_broadcast([P, P]), ident[:]
                )
            bias_tile = keep.tile([P, PAIR * N // 2], F32, name="bias_%d" % pair)
            nc.scalar.copy(out=bias_tile[:], in_=bank[:])
            bias_tiles[pair] = bias_tile

        def transpose_round(rnd):
            x_words = x_tiles[rnd][:].bitcast(F32)
            grouped = stage.tile([P, GROUP, P, PACK], BF16, align_bytes=64)
            for half in range(PAIRS_IN_GROUP):
                turned = turned_banks.tile([P, PAIR, 2, P], F32)
                for i in range(PAIR):
                    first_word = (half * PAIR + i) * WORDS
                    for u in range(2):
                        nc.tensor.transpose(
                            turned[:, i, u, :], x_words[:, first_word + u : first_word + WORDS : 2], ident[:]
                        )
                nc.scalar.copy(
                    out=grouped[:, half * PAIR : (half + 1) * PAIR, :, :].bitcast(F32),
                    in_=turned[:].rearrange("p i u row -> p i row u"),
                )
            grouped_tiles[rnd] = grouped

        def quantise_round(rnd):
            x_codes = stage.tile([P, GROUP * P], U32, align_bytes=64)
            x_planes = stage.tile([P, GROUP * P], U8, align_bytes=64)
            nc.vector.quantize_mx(
                out=x_codes[:].bitcast(FP8X4),
                scales=x_planes[:],
                in_=grouped_tiles[rnd][:].rearrange("p i row t -> p (i row t)"),
            )
            x_code_tiles[rnd] = x_codes
            x_plane_tiles[rnd] = x_planes

        def multiply_pair(rnd, half):
            group = rnd // ROW_TILES
            bias = bias_tiles[group * PAIRS_IN_GROUP + half][:].bitcast(BF16)
            if half == 0:
                result_tiles[rnd] = results.tile([P, GROUP * N], F32, name="result")
            for i in range(PAIR):
                in_group = half * PAIR + i
                mask = group * GROUP + in_group
                rows = slice(in_group * P, (in_group + 1) * P)
                product = product_banks.tile([P, N], F32)
                nc.tensor.matmul_mx(
                    out=product[:],
                    lhsT=x_code_tiles[rnd][:, rows].bitcast(FP8X4),
                    lhsT_scale=x_plane_tiles[rnd][:, rows],
                    rhs=w_tiles[group][:, in_group, :].bitcast(FP4X4),
                    rhs_scale=w_planes[mask // PLANE_MASKS][:, mask % PLANE_MASKS, :],
                    start=True,
                    stop=True,
                )
                nc.vector.tensor_tensor(
                    out=result_tiles[rnd][:, in_group * N : (in_group + 1) * N],
                    in0=product[:],
                    in1=bias[:, i * N : (i + 1) * N],
                    op=mybir.AluOpType.add,
                )

        def finish_round(rnd, stores):
            group, r = divmod(rnd, ROW_TILES)
            relus = max(stores, PAIRS_IN_GROUP)
            relu_width = GROUP * N // relus
            for piece in range(relus):
                values = result_tiles[rnd][:, piece * relu_width : (piece + 1) * relu_width]
                if piece * relu_width < PAIR * N:
                    nc.gpsimd.tensor_scalar(
                        out=values,
                        in0=values,
                        scalar1=float("inf"),
                        scalar2=0.0,
                        op0=mybir.AluOpType.min,
                        op1=mybir.AluOpType.max,
                    )
                else:
                    nc.scalar.activation(out=values, in_=values, func=mybir.ActivationFunctionType.Relu)
            store_width = GROUP * N // stores
            for piece in range(stores):
                cols = slice(piece * store_width, (piece + 1) * store_width)
                first_col = group * GROUP * N + piece * store_width
                nc.sync.dma_start(
                    out=out[r * P : (r + 1) * P, first_col : first_col + store_width], in_=result_tiles[rnd][:, cols]
                )

        assert PAIRS == ROUNDS
        turn_bias()
        broadcast_bias(0)
        for step in range(ROUNDS + 2):
            if step < ROUNDS:
                transpose_round(step)
            if step >= 2:
                finish_round(step - 2, stores=GROUP if step - 2 == ROUNDS - 1 else 1)
            if 1 <= step <= ROUNDS:
                multiply_pair(step - 1, 0)
            if step < ROUNDS:
                quantise_round(step)
            if step + 1 < PAIRS:
                broadcast_bias(step + 1)
            if 1 <= step <= ROUNDS:
                multiply_pair(step - 1, 1)
